import numpy as np
import ml_dtypes


def mxq(x, axis, fmt="e4m3"):
    dtype, down = {"e4m3": (ml_dtypes.float8_e4m3fn, 7), "e5m2": (ml_dtypes.float8_e5m2, 14)}[fmt]
    v = np.moveaxis(np.asarray(x, np.float32).astype(ml_dtypes.bfloat16).astype(np.float64), axis, -1)
    blocks = v.reshape(v.shape[:-1] + (-1, 32))
    amax = np.abs(blocks).max(-1, keepdims=True)
    byte = np.maximum(np.where(amax > 0, np.frexp(amax)[1] - 1 + 127, 0) - down, 1)
    scale = np.exp2(byte - 127.0)
    codes = (blocks / scale).astype(np.float32).astype(dtype).astype(np.float64)
    return np.moveaxis((codes * scale).reshape(v.shape), -1, axis)


WIDE = False


def mx_kscale(k):
    if not WIDE:
        return np.ones(k)
    levels = np.array([30, -30])
    if k % 512:
        return np.exp2(np.random.permutation(np.resize(levels, k // 32))).repeat(32)
    a = np.empty((k // 512, 16))
    for p in range(k // 512):
        a[p, :8] = np.random.permutation(np.resize(levels, 8))
        for g in range(8):
            far = levels[np.abs(levels - a[p, g]) >= 10]
            a[p, g + 8] = far[np.random.randint(len(far))]
    return np.exp2(a.ravel()).repeat(32)


BF16 = ml_dtypes.bfloat16


def bf(x):
    return np.asarray(x, np.float32).astype(BF16)


def f64(x):
    return np.asarray(x).astype(np.float64)


E2M1 = np.array([0.0, 0.5, 1.0, 1.5, 2.0, 3.0, 4.0, 6.0, -0.0, -0.5, -1.0, -1.5, -2.0, -3.0, -4.0, -6.0])


def pack_weight(w, fmt):
    k, n = w.shape
    w = f64(bf(w)).reshape(k // 32, 32, n)
    amax = np.abs(w).max(1)
    if fmt == "e4m3":
        byte = np.frexp(amax)[1] - 1 + 127 - 7
    else:
        mant, ex = np.frexp(amax / 6.0)
        byte = np.where(mant > 0.5, ex, ex - 1) + 127
    byte = np.clip(np.where(amax > 0, byte, 1), 1, 254)
    scaled = (w * np.exp2(127.0 - byte)[:, None, :]).reshape(k, n).astype(np.float32)
    by_word = np.ascontiguousarray(scaled.reshape(k // 512, 128, 4, n).transpose(0, 1, 3, 2))
    if fmt == "e4m3":
        words = by_word.astype(ml_dtypes.float8_e4m3fn).view(np.uint8)
    else:
        c = by_word.astype(ml_dtypes.float4_e2m1fn).view(np.uint8) & 0xF
        words = c[..., 0::2] | (c[..., 1::2] << 4)
    return np.ascontiguousarray(words), np.ascontiguousarray(byte.astype(np.uint8).reshape(k // 512, 16, n))


def unpack_weight(words, scales, fmt):
    g, p, n, _ = words.shape
    if fmt == "e4m3":
        vals = np.ascontiguousarray(words).view(ml_dtypes.float8_e4m3fn).astype(np.float64)
    else:
        nib = np.empty((g, p, n, 4), np.uint8)
        nib[..., 0::2] = words & 0xF
        nib[..., 1::2] = words >> 4
        vals = E2M1[nib]
    vals = vals * np.repeat(np.exp2(scales.astype(np.float64) - 127.0), 8, axis=1)[..., None]
    return vals.transpose(0, 1, 3, 2).reshape(g * 512, n)

def pack4(w):
    words, scales = pack_weight(w, "e2m1")
    return words.reshape(words.shape[0], 128, -1), scales


def unpack4(words, scales):
    return unpack_weight(words.reshape(words.shape[0], 128, -1, 2), scales, "e2m1")


B, S, IN, OUT, A, R = 8, 128, 2048, 2048, 8, 128
G = B // A
SCALING = 2.0


def setup_inputs():
    s = mx_kscale(IN)
    data = bf(np.random.standard_normal((B, S, IN)) * s)
    w = np.random.standard_normal((OUT, IN)) / np.sqrt(IN) / s
    W_words, W_scales = pack4(np.ascontiguousarray(w.T))
    t_lora = bf(np.random.standard_normal((A, G, S, R)))
    lora_b = bf(np.random.standard_normal((A, OUT, R)) * 0.5 / np.sqrt(R))
    return {"data": data,
            "W_words": W_words,
            "W_scales": W_scales,
            "t_lora": t_lora,
            "lora_b": lora_b}


def reference(data, W_words, W_scales, t_lora, lora_b):
    base = mxq(f64(data), 2, "e5m2") @ unpack4(W_words, W_scales)
    delta = (f64(t_lora).reshape(A, G * S, R) @ f64(lora_b).transpose(0, 2, 1)) * SCALING
    return base + delta.reshape(B, S, OUT)

@@ -1,0 +1,261 @@
+from contextlib import ExitStack
+
+import concourse.mybir as mybir
+from concourse.masks import make_identity
+
+B, S, IN, OUT, R = 8, 128, 2048, 2048, 128
+SCALING = 2.0
+FLOPS = 2 * B * S * IN * OUT + 2 * B * S * R * OUT
+
+F32 = mybir.dt.float32
+BF16 = mybir.dt.bfloat16
+I32 = mybir.dt.int32
+U32 = mybir.dt.uint32
+U8 = mybir.dt.uint8
+E5M2X4 = mybir.dt.float8_e5m2_x4
+E2M1X4 = mybir.dt.float4_e2m1fn_x4
+
+P = 128
+PASSES = IN // 512
+N_TILE = 512
+CHUNKS = OUT // N_TILE
+HALVES = 2
+HALF = 1024
+BANKS = 8
+PER_BANK = 4
+
+
+def tile_linear_pa_kernel(tc, data, W_words, W_scales, t_lora, lora_b, out):
+    nc = tc.nc
+    with ExitStack() as ctx:
+        keep = ctx.enter_context(tc.tile_pool(name="keep", bufs=1))
+        stage = ctx.enter_context(tc.tile_pool(name="stage", bufs=4))
+        psum = ctx.enter_context(tc.psum_pool(name="psum", bufs=1))
+        ctx.enter_context(tc.manual_schedule())
+
+        banks_taken = []
+
+        def next_bank(width, dtype):
+            tag = "bank%d" % (len(banks_taken) % BANKS)
+            bank = psum.tile([P, width], dtype, name=tag, tag=tag)
+            banks_taken.append(tag)
+            return bank
+
+        ident_f32 = keep.tile([P, P], F32, name="ident_f32")
+        ident_bf16 = keep.tile([P, P], BF16, name="ident_bf16")
+        make_identity(nc, ident_f32[:])
+        make_identity(nc, ident_bf16[:])
+
+        x_raw, b_raw, w_codes, w_scales = {}, {}, {}, {}
+        x_split, b_paired, x_grouped, x_codes, x_scales, b_T, delta = {}, {}, {}, {}, {}, {}, {}
+
+        def load_x(b):
+            tile = keep.tile([P, IN], BF16, name="x_raw%d" % b)
+            nc.sync.dma_start(out=tile[:], in_=data[b])
+            for h in range(HALVES):
+                x_raw[b, h] = tile[:, h * HALF : (h + 1) * HALF]
+
+        def load_b(b):
+            tile = keep.tile([P, HALVES, HALF], BF16, name="b_raw%d" % b)
+            nc.sync.dma_start(out=tile[:], in_=lora_b[b].rearrange("(h p x) r -> p h (x r)", h=HALVES, p=P))
+            for h in range(HALVES):
+                b_raw[b, h] = tile[:, h, :]
+
+        def load_b_by_halves(b):
+            rows = lora_b[b].rearrange("(h p x) r -> h p (x r)", h=HALVES, p=P)
+            for h in range(HALVES):
+                tile = keep.tile([P, HALF], BF16, name="b_raw%d_%d" % (b, h))
+                nc.sync.dma_start(out=tile[:], in_=rows[h])
+                b_raw[b, h] = tile[:]
+
+        def load_w(n):
+            plane = keep.tile([P, PASSES, N_TILE], U8, name="w_scales%d" % n, align_bytes=64)
+            cols = slice(n * N_TILE, (n + 1) * N_TILE)
+            for r in range(4):
+                nc.sync.dma_start(
+                    out=plane[r:P:32, :, :].bitcast(I32),
+                    in_=W_scales[:, r:16:4, cols].rearrange("g q n -> q g n").bitcast(I32),
+                )
+            words = keep.tile([P, PASSES, 2 * N_TILE], U8, name="w_codes%d" % n, align_bytes=64)
+            nc.sync.dma_start(
+                out=words[:].bitcast(I32),
+                in_=W_words[:, :, 2 * n * N_TILE : 2 * (n + 1) * N_TILE].rearrange("g p c -> p g c").bitcast(I32),
+            )
+            w_scales[n], w_codes[n] = plane, words
+
+        load_b_by_halves(0)
+        t_raw = keep.tile([P, B, R], BF16, name="t_raw")
+        nc.sync.dma_start(out=t_raw[:], in_=t_lora.rearrange("a g s r -> s (a g) r"))
+        load_x(0)
+        load_w(0)
+        load_x(1)
+        load_b(1)
+        for n in range(1, CHUNKS):
+            load_w(n)
+        for b in range(2, B):
+            load_b(b)
+            load_x(b)
+
+        def split_x(b):
+            for h in range(HALVES):
+                tile = stage.tile([P, HALF // 2], F32, name="x_split", tag="x_split")
+                nc.vector.tensor_copy(
+                    out=tile[:].rearrange("s (g u p) -> s g u p", g=2, u=2),
+                    in_=x_raw[b, h].bitcast(F32).rearrange("s (g p u) -> s g u p", g=2, u=2),
+                )
+                x_split[b, h] = tile
+
+        def pair_b(b):
+            for h in range(HALVES):
+                tile = stage.tile([P, HALF], BF16, name="b_paired", tag="b_paired")
+                nc.vector.tensor_copy(
+                    out=tile[:].rearrange("p (y r j) -> p y r j", y=PER_BANK, j=2),
+                    in_=b_raw[b, h].rearrange("p (y j r) -> p y r j", y=PER_BANK, j=2),
+                )
+                b_paired[b, h] = tile
+
+        def transpose_words(words):
+            bank = next_bank(PER_BANK * P, F32)
+            for i in range(PER_BANK):
+                nc.tensor.transpose(bank[:, i * P : (i + 1) * P], words[:, i * P : (i + 1) * P], ident_f32[:])
+            return bank
+
+        def transpose_x(b, h):
+            bank = transpose_words(x_split[b, h][:])
+            tile = stage.tile([P, HALF], BF16, name="x_grouped", tag="x_grouped", align_bytes=64)
+            nc.scalar.copy(
+                out=tile[:].bitcast(F32).rearrange("p (g s u) -> p g s u", g=2, u=2),
+                in_=bank[:].rearrange("p (g u s) -> p g s u", g=2, u=2),
+            )
+            x_grouped[b, h] = tile
+
+        def transpose_b(b, h):
+            bank = transpose_words(b_paired[b, h][:].bitcast(F32))
+            tile = stage.tile([P, HALF], BF16, name="b_T", tag="b_T")
+            nc.scalar.copy(
+                out=tile[:].bitcast(F32).rearrange("r (p y) -> r p y", y=PER_BANK),
+                in_=bank[:].rearrange("r (y p) -> r p y", y=PER_BANK),
+            )
+            b_T[b, h] = tile
+
+        def quantize_x(b, h):
+            codes = stage.tile([P, HALF // 4], U32, name="x_codes", tag="x_codes", align_bytes=64)
+            scales = stage.tile([P, HALF // 4], U8, name="x_scales", tag="x_scales", align_bytes=64)
+            nc.vector.quantize_mx(out=codes[:].bitcast(E5M2X4), scales=scales[:], in_=x_grouped[b, h][:])
+            x_codes[b, h], x_scales[b, h] = codes, scales
+
+        t_T = keep.tile([P, B * S], BF16, name="t_T")
+
+        def transpose_t():
+            bank = next_bank(B * S, BF16)
+            for a in range(B):
+                nc.tensor.transpose(bank[:, a * S : (a + 1) * S], t_raw[:, a, :], ident_bf16[:])
+            nc.scalar.copy(out=t_T[:], in_=bank[:])
+
+        def lora_product(b, n):
+            bank = next_bank(N_TILE, F32)
+            h, c = divmod(n, 2)
+            nc.tensor.matmul(
+                bank[:],
+                lhsT=t_T[:, b * S : (b + 1) * S],
+                rhs=b_T[b, h][:, c * N_TILE : (c + 1) * N_TILE],
+                start=True,
+                stop=True,
+            )
+            tile = stage.tile([P, N_TILE], F32, name="delta", tag="delta", bufs=8)
+            nc.scalar.copy(out=tile[:], in_=bank[:])
+            delta[b, n] = tile
+
+        def base_product(b, n, lo, hi):
+            bank = next_bank(hi - lo, F32)
+            for g in range(PASSES):
+                h, c = divmod(g, 2)
+                cols = slice(c * S, (c + 1) * S)
+                nc.tensor.matmul_mx(
+                    out=bank[:],
+                    lhsT=x_codes[b, h][:, cols].bitcast(E5M2X4),
+                    lhsT_scale=x_scales[b, h][:, cols],
+                    rhs=w_codes[n][:, g, 2 * lo : 2 * hi].bitcast(E2M1X4),
+                    rhs_scale=w_scales[n][:, g, lo:hi],
+                    start=(g == 0),
+                    stop=(g == PASSES - 1),
+                )
+            return bank
+
+        def finish(b, n, lo, hi, bank):
+            result = stage.tile([P, hi - lo], F32, name="result", tag="result", bufs=16)
+            nc.vector.scalar_tensor_tensor(
+                out=result[:],
+                in0=delta[b, n][:, lo:hi],
+                scalar=SCALING,
+                in1=bank[:],
+                op0=mybir.AluOpType.mult,
+                op1=mybir.AluOpType.add,
+            )
+            nc.sync.dma_start(out=out[b, :, n * N_TILE + lo : n * N_TILE + hi], in_=result[:])
+
+        def multiply(b, n):
+            last = (b, n) == (B - 1, CHUNKS - 1)
+            width = N_TILE // 2 if last else N_TILE
+            for lo in range(0, N_TILE, width):
+                finish(b, n, lo, lo + width, base_product(b, n, lo, lo + width))
+
+        pair_b(0)
+        transpose_b(0, 0)
+        transpose_t()
+        transpose_b(0, 1)
+        split_x(0)
+        for h in range(HALVES):
+            transpose_x(0, h)
+        for n in range(CHUNKS):
+            lora_product(0, n)
+        for h in range(HALVES):
+            quantize_x(0, h)
+        split_x(1)
+        pair_b(1)
+        multiply(0, 0)
+        for h in range(HALVES):
+            transpose_x(1, h)
+        for h in range(HALVES):
+            transpose_b(1, h)
+        for h in range(HALVES):
+            quantize_x(1, h)
+        multiply(0, 1)
+        for n in range(CHUNKS):
+            lora_product(1, n)
+        multiply(0, 2)
+        multiply(1, 0)
+        pair_b(2)
+        multiply(0, 3)
+        split_x(2)
+        multiply(1, 1)
+        for h in range(HALVES):
+            transpose_b(2, h)
+            transpose_x(2, h)
+        pair_b(3)
+        multiply(1, 2)
+        split_x(3)
+        for h in range(HALVES):
+            quantize_x(2, h)
+        multiply(1, 3)
+
+        for b in range(2, B):
+            ahead = b + 1 < B
+            for h in range(HALVES):
+                lora_product(b, 2 * h)
+                if ahead:
+                    transpose_b(b + 1, h)
+                lora_product(b, 2 * h + 1)
+                if ahead:
+                    transpose_x(b + 1, h)
+            if b + 2 < B:
+                pair_b(b + 2)
+                split_x(b + 2)
+            if ahead:
+                quantize_x(b + 1, 0)
+            multiply(b, 0)
+            multiply(b, 1)
+            if ahead:
+                quantize_x(b + 1, 1)
+            multiply(b, 2)
+            multiply(b, 3)

@@ -1,4 +1,5 @@
 from contextlib import ExitStack
+from functools import partial
 
 import concourse.mybir as mybir
 from concourse.masks import make_identity
@@ -23,6 +24,7 @@ HALVES = 2
 HALF = 1024
 BANKS = 8
 PER_BANK = 4
+PIECE = 256
 
 
 def tile_linear_pa_kernel(tc, data, W_words, W_scales, t_lora, lora_b, out):
@@ -46,7 +48,7 @@ def tile_linear_pa_kernel(tc, data, W_words, W_scales, t_lora, lora_b, out):
         make_identity(nc, ident_f32[:])
         make_identity(nc, ident_bf16[:])
 
-        x_raw, b_raw, w_codes, w_scales = {}, {}, {}, {}
+        x_raw, b_raw, t_raw, t_T, w_codes, w_scales = {}, {}, {}, {}, {}, {}
         x_split, b_paired, x_grouped, x_codes, x_scales, b_T, delta = {}, {}, {}, {}, {}, {}, {}
 
         def load_x(b):
@@ -83,17 +85,23 @@ def tile_linear_pa_kernel(tc, data, W_words, W_scales, t_lora, lora_b, out):
             )
             w_scales[n], w_codes[n] = plane, words
 
+        def load_t(b):
+            tile = keep.tile([P, R], BF16, name="t_raw%d" % b)
+            nc.sync.dma_start(out=tile[:], in_=t_lora[b, 0])
+            t_raw[b] = tile
+
         load_b_by_halves(0)
-        t_raw = keep.tile([P, B, R], BF16, name="t_raw")
-        nc.sync.dma_start(out=t_raw[:], in_=t_lora.rearrange("a g s r -> s (a g) r"))
+        load_t(0)
         load_x(0)
+        load_b(1)
+        load_t(1)
         load_w(0)
         load_x(1)
-        load_b(1)
         for n in range(1, CHUNKS):
             load_w(n)
         for b in range(2, B):
             load_b(b)
+            load_t(b)
             load_x(b)
 
         def split_x(b):
@@ -114,29 +122,50 @@ def tile_linear_pa_kernel(tc, data, W_words, W_scales, t_lora, lora_b, out):
                 )
                 b_paired[b, h] = tile
 
-        def transpose_words(words):
-            bank = next_bank(PER_BANK * P, F32)
-            for i in range(PER_BANK):
+        def word_transposes(words, empty):
+            taken = []
+
+            def step(i):
+                if i == 0:
+                    taken.append(next_bank(PER_BANK * P, F32))
+                bank = taken[0]
                 nc.tensor.transpose(bank[:, i * P : (i + 1) * P], words[:, i * P : (i + 1) * P], ident_f32[:])
-            return bank
+                if i == PER_BANK - 1:
+                    empty(bank)
 
-        def transpose_x(b, h):
-            bank = transpose_words(x_split[b, h][:])
-            tile = stage.tile([P, HALF], BF16, name="x_grouped", tag="x_grouped", align_bytes=64)
-            nc.scalar.copy(
-                out=tile[:].bitcast(F32).rearrange("p (g s u) -> p g s u", g=2, u=2),
-                in_=bank[:].rearrange("p (g u s) -> p g s u", g=2, u=2),
-            )
-            x_grouped[b, h] = tile
+            return [partial(step, i) for i in range(PER_BANK)]
 
-        def transpose_b(b, h):
-            bank = transpose_words(b_paired[b, h][:].bitcast(F32))
-            tile = stage.tile([P, HALF], BF16, name="b_T", tag="b_T")
-            nc.scalar.copy(
-                out=tile[:].bitcast(F32).rearrange("r (p y) -> r p y", y=PER_BANK),
-                in_=bank[:].rearrange("r (y p) -> r p y", y=PER_BANK),
-            )
-            b_T[b, h] = tile
+        def transposes_x(b, h):
+            def empty(bank):
+                tile = stage.tile([P, HALF], BF16, name="x_grouped", tag="x_grouped", align_bytes=64)
+                nc.scalar.copy(
+                    out=tile[:].bitcast(F32).rearrange("p (g s u) -> p g s u", g=2, u=2),
+                    in_=bank[:].rearrange("p (g u s) -> p g s u", g=2, u=2),
+                )
+                x_grouped[b, h] = tile
+
+            return word_transposes(x_split[b, h][:], empty)
+
+        def transposes_b(b, h):
+            def empty(bank):
+                tile = stage.tile([P, HALF], BF16, name="b_T", tag="b_T")
+                nc.scalar.copy(
+                    out=tile[:].bitcast(F32).rearrange("r (p y) -> r p y", y=PER_BANK),
+                    in_=bank[:].rearrange("r (y p) -> r p y", y=PER_BANK),
+                )
+                b_T[b, h] = tile
+
+            return word_transposes(b_paired[b, h][:].bitcast(F32), empty)
+
+        def transposes_t(b):
+            def step():
+                bank = next_bank(S, BF16)
+                nc.tensor.transpose(bank[:], t_raw[b][:], ident_bf16[:])
+                tile = stage.tile([P, S], BF16, name="t_T", tag="t_T")
+                nc.scalar.copy(out=tile[:], in_=bank[:])
+                t_T[b] = tile
+
+            return [step]
 
         def quantize_x(b, h):
             codes = stage.tile([P, HALF // 4], U32, name="x_codes", tag="x_codes", align_bytes=64)
@@ -144,27 +173,44 @@ def tile_linear_pa_kernel(tc, data, W_words, W_scales, t_lora, lora_b, out):
             nc.vector.quantize_mx(out=codes[:].bitcast(E5M2X4), scales=scales[:], in_=x_grouped[b, h][:])
             x_codes[b, h], x_scales[b, h] = codes, scales
 
-        t_T = keep.tile([P, B * S], BF16, name="t_T")
-
-        def transpose_t():
-            bank = next_bank(B * S, BF16)
-            for a in range(B):
-                nc.tensor.transpose(bank[:, a * S : (a + 1) * S], t_raw[:, a, :], ident_bf16[:])
-            nc.scalar.copy(out=t_T[:], in_=bank[:])
-
-        def lora_product(b, n):
-            bank = next_bank(N_TILE, F32)
-            h, c = divmod(n, 2)
-            nc.tensor.matmul(
-                bank[:],
-                lhsT=t_T[:, b * S : (b + 1) * S],
-                rhs=b_T[b, h][:, c * N_TILE : (c + 1) * N_TILE],
-                start=True,
-                stop=True,
-            )
+        def empty_lora(b, n, bank, copy):
             tile = stage.tile([P, N_TILE], F32, name="delta", tag="delta", bufs=8)
-            nc.scalar.copy(out=tile[:], in_=bank[:])
+            copy(out=tile[:], in_=bank[:])
             delta[b, n] = tile
+
+        def lora_pieces(b, n, empty):
+            taken = []
+            h, c = divmod(n, 2)
+
+            def step(i):
+                if i == 0:
+                    taken.append(next_bank(N_TILE, F32))
+                bank = taken[0]
+                lo = i * PIECE
+                nc.tensor.matmul(
+                    bank[:, lo : lo + PIECE],
+                    lhsT=t_T[b][:],
+                    rhs=b_T[b, h][:, c * N_TILE + lo : c * N_TILE + lo + PIECE],
+                    start=True,
+                    stop=True,
+                )
+                if lo + PIECE == N_TILE:
+                    empty(bank)
+
+            return [partial(step, i) for i in range(N_TILE // PIECE)]
+
+        def lora_steps(b, chunks):
+            steps = []
+            for n in chunks:
+                steps += lora_pieces(b, n, partial(empty_lora, b, n, copy=nc.scalar.copy))
+            return steps
+
+        def weave(matmuls, transposes, gaps):
+            for i, matmul in enumerate(matmuls):
+                matmul()
+                if i < gaps:
+                    for step in transposes[i * len(transposes) // gaps : (i + 1) * len(transposes) // gaps]:
+                        step()
 
         def base_product(b, n, lo, hi):
             bank = next_bank(hi - lo, F32)
@@ -200,40 +246,43 @@ def tile_linear_pa_kernel(tc, data, W_words, W_scales, t_lora, lora_b, out):
             for lo in range(0, N_TILE, width):
                 finish(b, n, lo, lo + width, base_product(b, n, lo, lo + width))
 
+        def transposes_row(b):
+            return transposes_b(b, 0) + transposes_t(b) + transposes_x(b, 0) + transposes_b(b, 1) + transposes_x(b, 1)
+
         pair_b(0)
-        transpose_b(0, 0)
-        transpose_t()
-        transpose_b(0, 1)
+        for step in transposes_b(0, 0) + transposes_t(0) + transposes_b(0, 1):
+            step()
         split_x(0)
-        for h in range(HALVES):
-            transpose_x(0, h)
-        for n in range(CHUNKS):
-            lora_product(0, n)
+        late = {}
+        steps = lora_steps(0, [0])
+        for n in (1, 2, 3):
+            steps += lora_pieces(0, n, partial(late.setdefault, n))
+        weave(steps, transposes_x(0, 0) + transposes_x(0, 1), 3)
+        pair_b(1)
+        for step in transposes_b(1, 0) + transposes_t(1) + transposes_b(1, 1):
+            step()
         for h in range(HALVES):
             quantize_x(0, h)
+        empty_lora(0, 1, late[1], nc.vector.tensor_copy)
+        empty_lora(0, 2, late[2], nc.vector.tensor_copy)
+        empty_lora(0, 3, late[3], nc.scalar.copy)
+        weave(lora_steps(1, [0]), [], 0)
         split_x(1)
-        pair_b(1)
         multiply(0, 0)
-        for h in range(HALVES):
-            transpose_x(1, h)
-        for h in range(HALVES):
-            transpose_b(1, h)
+        weave(lora_steps(1, [1, 2, 3]), transposes_x(1, 0) + transposes_x(1, 1), 3)
         for h in range(HALVES):
             quantize_x(1, h)
         multiply(0, 1)
-        for n in range(CHUNKS):
-            lora_product(1, n)
-        multiply(0, 2)
         multiply(1, 0)
-        pair_b(2)
-        multiply(0, 3)
-        split_x(2)
         multiply(1, 1)
-        for h in range(HALVES):
-            transpose_b(2, h)
-            transpose_x(2, h)
-        pair_b(3)
+        multiply(0, 2)
+        pair_b(2)
         multiply(1, 2)
+        split_x(2)
+        multiply(0, 3)
+        for step in transposes_row(2):
+            step()
+        pair_b(3)
         split_x(3)
         for h in range(HALVES):
             quantize_x(2, h)
@@ -241,13 +290,8 @@ def tile_linear_pa_kernel(tc, data, W_words, W_scales, t_lora, lora_b, out):
 
         for b in range(2, B):
             ahead = b + 1 < B
-            for h in range(HALVES):
-                lora_product(b, 2 * h)
-                if ahead:
-                    transpose_b(b + 1, h)
-                lora_product(b, 2 * h + 1)
-                if ahead:
-                    transpose_x(b + 1, h)
+            steps = lora_steps(b, range(CHUNKS))
+            weave(steps, transposes_row(b + 1) if ahead else [], len(steps) - 1)
             if b + 2 < B:
                 pair_b(b + 2)
                 split_x(b + 2)

@@ -24,7 +24,7 @@ HALVES = 2
 HALF = 1024
 BANKS = 8
 PER_BANK = 4
-PIECE = 256
+TAIL_WIDTHS = (256, 256)
 
 
 def tile_linear_pa_kernel(tc, data, W_words, W_scales, t_lora, lora_b, out):
@@ -49,7 +49,7 @@ def tile_linear_pa_kernel(tc, data, W_words, W_scales, t_lora, lora_b, out):
         make_identity(nc, ident_bf16[:])
 
         x_raw, b_raw, t_raw, t_T, w_codes, w_scales = {}, {}, {}, {}, {}, {}
-        x_split, b_paired, x_grouped, x_codes, x_scales, b_T, delta = {}, {}, {}, {}, {}, {}, {}
+        x_split, b_paired, x_grouped, x_codes, x_scales, b_T, waiting = {}, {}, {}, {}, {}, {}, {}
 
         def load_x(b):
             tile = keep.tile([P, IN], BF16, name="x_raw%d" % b)
@@ -57,18 +57,17 @@ def tile_linear_pa_kernel(tc, data, W_words, W_scales, t_lora, lora_b, out):
             for h in range(HALVES):
                 x_raw[b, h] = tile[:, h * HALF : (h + 1) * HALF]
 
+        def load_x_by_halves(b):
+            for h in range(HALVES):
+                tile = keep.tile([P, HALF], BF16, name="x_raw%d_%d" % (b, h))
+                nc.sync.dma_start(out=tile[:], in_=data[b, :, h * HALF : (h + 1) * HALF])
+                x_raw[b, h] = tile[:]
+
         def load_b(b):
             tile = keep.tile([P, HALVES, HALF], BF16, name="b_raw%d" % b)
             nc.sync.dma_start(out=tile[:], in_=lora_b[b].rearrange("(h p x) r -> p h (x r)", h=HALVES, p=P))
             for h in range(HALVES):
                 b_raw[b, h] = tile[:, h, :]
-
-        def load_b_by_halves(b):
-            rows = lora_b[b].rearrange("(h p x) r -> h p (x r)", h=HALVES, p=P)
-            for h in range(HALVES):
-                tile = keep.tile([P, HALF], BF16, name="b_raw%d_%d" % (b, h))
-                nc.sync.dma_start(out=tile[:], in_=rows[h])
-                b_raw[b, h] = tile[:]
 
         def load_w(n):
             plane = keep.tile([P, PASSES, N_TILE], U8, name="w_scales%d" % n, align_bytes=64)
@@ -90,19 +89,22 @@ def tile_linear_pa_kernel(tc, data, W_words, W_scales, t_lora, lora_b, out):
             nc.sync.dma_start(out=tile[:], in_=t_lora[b, 0])
             t_raw[b] = tile
 
-        load_b_by_halves(0)
+        load_x_by_halves(0)
+        load_x(1)
+        load_w(0)
+        load_w(1)
+        load_b(0)
         load_t(0)
-        load_x(0)
+        load_w(2)
         load_b(1)
         load_t(1)
-        load_w(0)
-        load_x(1)
-        for n in range(1, CHUNKS):
-            load_w(n)
+        load_x(2)
+        load_w(3)
         for b in range(2, B):
             load_b(b)
             load_t(b)
-            load_x(b)
+            if b + 1 < B:
+                load_x(b + 1)
 
         def split_x(b):
             for h in range(HALVES):
@@ -173,37 +175,38 @@ def tile_linear_pa_kernel(tc, data, W_words, W_scales, t_lora, lora_b, out):
             nc.vector.quantize_mx(out=codes[:].bitcast(E5M2X4), scales=scales[:], in_=x_grouped[b, h][:])
             x_codes[b, h], x_scales[b, h] = codes, scales
 
-        def empty_lora(b, n, bank, copy):
-            tile = stage.tile([P, N_TILE], F32, name="delta", tag="delta", bufs=8)
-            copy(out=tile[:], in_=bank[:])
-            delta[b, n] = tile
+        def deliver(b, n, lo, hi, bank, is_lora):
+            if (b, n) not in waiting:
+                tile = stage.tile([P, N_TILE], F32, name="waiting", tag="waiting", bufs=10)
+                nc.scalar.copy(out=tile[:], in_=bank[:])
+                waiting[b, n] = tile
+                return
+            other = waiting[b, n][:, lo:hi]
+            result = stage.tile([P, hi - lo], F32, name="result", tag="result", bufs=16)
+            nc.vector.scalar_tensor_tensor(
+                out=result[:],
+                in0=bank[:] if is_lora else other,
+                scalar=SCALING,
+                in1=other if is_lora else bank[:],
+                op0=mybir.AluOpType.mult,
+                op1=mybir.AluOpType.add,
+            )
+            nc.sync.dma_start(out=out[b, :, n * N_TILE + lo : n * N_TILE + hi], in_=result[:])
 
-        def lora_pieces(b, n, empty):
-            taken = []
+        def lora_product(b, n):
+            bank = next_bank(N_TILE, F32)
             h, c = divmod(n, 2)
+            nc.tensor.matmul(
+                bank[:],
+                lhsT=t_T[b][:],
+                rhs=b_T[b, h][:, c * N_TILE : (c + 1) * N_TILE],
+                start=True,
+                stop=True,
+            )
+            deliver(b, n, 0, N_TILE, bank, True)
 
-            def step(i):
-                if i == 0:
-                    taken.append(next_bank(N_TILE, F32))
-                bank = taken[0]
-                lo = i * PIECE
-                nc.tensor.matmul(
-                    bank[:, lo : lo + PIECE],
-                    lhsT=t_T[b][:],
-                    rhs=b_T[b, h][:, c * N_TILE + lo : c * N_TILE + lo + PIECE],
-                    start=True,
-                    stop=True,
-                )
-                if lo + PIECE == N_TILE:
-                    empty(bank)
-
-            return [partial(step, i) for i in range(N_TILE // PIECE)]
-
-        def lora_steps(b, chunks):
-            steps = []
-            for n in chunks:
-                steps += lora_pieces(b, n, partial(empty_lora, b, n, copy=nc.scalar.copy))
-            return steps
+        def lora_steps(b):
+            return [partial(lora_product, b, n) for n in range(CHUNKS)]
 
         def weave(matmuls, transposes, gaps):
             for i, matmul in enumerate(matmuls):
@@ -228,78 +231,66 @@ def tile_linear_pa_kernel(tc, data, W_words, W_scales, t_lora, lora_b, out):
                 )
             return bank
 
-        def finish(b, n, lo, hi, bank):
-            result = stage.tile([P, hi - lo], F32, name="result", tag="result", bufs=16)
-            nc.vector.scalar_tensor_tensor(
-                out=result[:],
-                in0=delta[b, n][:, lo:hi],
-                scalar=SCALING,
-                in1=bank[:],
-                op0=mybir.AluOpType.mult,
-                op1=mybir.AluOpType.add,
-            )
-            nc.sync.dma_start(out=out[b, :, n * N_TILE + lo : n * N_TILE + hi], in_=result[:])
-
         def multiply(b, n):
-            last = (b, n) == (B - 1, CHUNKS - 1)
-            width = N_TILE // 2 if last else N_TILE
-            for lo in range(0, N_TILE, width):
-                finish(b, n, lo, lo + width, base_product(b, n, lo, lo + width))
+            widths = TAIL_WIDTHS if (b, n) == (B - 1, CHUNKS - 1) else (N_TILE,)
+            lo = 0
+            for width in widths:
+                deliver(b, n, lo, lo + width, base_product(b, n, lo, lo + width), False)
+                lo += width
 
-        def transposes_row(b):
-            return transposes_b(b, 0) + transposes_t(b) + transposes_x(b, 0) + transposes_b(b, 1) + transposes_x(b, 1)
+        def run(steps):
+            for step in steps:
+                step()
 
-        pair_b(0)
-        for step in transposes_b(0, 0) + transposes_t(0) + transposes_b(0, 1):
-            step()
+        def plain_stretch(b):
+            transposes = transposes_b(b, 0) + transposes_t(b)
+            if b + 1 < B:
+                transposes += transposes_x(b + 1, 0)
+            transposes += transposes_b(b, 1)
+            if b + 1 < B:
+                transposes += transposes_x(b + 1, 1)
+            weave(lora_steps(b - 1), transposes, CHUNKS - 1)
+
+        def prepare(b):
+            pair_b(b)
+            if b + 1 < B:
+                split_x(b + 1)
+
         split_x(0)
-        late = {}
-        steps = lora_steps(0, [0])
-        for n in (1, 2, 3):
-            steps += lora_pieces(0, n, partial(late.setdefault, n))
-        weave(steps, transposes_x(0, 0) + transposes_x(0, 1), 3)
-        pair_b(1)
-        for step in transposes_b(1, 0) + transposes_t(1) + transposes_b(1, 1):
-            step()
-        for h in range(HALVES):
-            quantize_x(0, h)
-        empty_lora(0, 1, late[1], nc.vector.tensor_copy)
-        empty_lora(0, 2, late[2], nc.vector.tensor_copy)
-        empty_lora(0, 3, late[3], nc.scalar.copy)
-        weave(lora_steps(1, [0]), [], 0)
+        run(transposes_x(0, 0) + transposes_x(0, 1))
         split_x(1)
+        run(transposes_x(1, 0) + transposes_x(1, 1))
+        for b in range(2):
+            for h in range(HALVES):
+                quantize_x(b, h)
         multiply(0, 0)
-        weave(lora_steps(1, [1, 2, 3]), transposes_x(1, 0) + transposes_x(1, 1), 3)
-        for h in range(HALVES):
-            quantize_x(1, h)
-        multiply(0, 1)
         multiply(1, 0)
+        pair_b(0)
+        multiply(0, 1)
         multiply(1, 1)
+        run(transposes_b(0, 0) + transposes_t(0) + transposes_b(0, 1))
+        prepare(1)
         multiply(0, 2)
-        pair_b(2)
         multiply(1, 2)
-        split_x(2)
+        plain_stretch(1)
+        prepare(2)
         multiply(0, 3)
-        for step in transposes_row(2):
-            step()
-        pair_b(3)
-        split_x(3)
         for h in range(HALVES):
             quantize_x(2, h)
         multiply(1, 3)
 
-        for b in range(2, B):
-            ahead = b + 1 < B
-            steps = lora_steps(b, range(CHUNKS))
-            weave(steps, transposes_row(b + 1) if ahead else [], len(steps) - 1)
-            if b + 2 < B:
-                pair_b(b + 2)
-                split_x(b + 2)
-            if ahead:
-                quantize_x(b + 1, 0)
-            multiply(b, 0)
-            multiply(b, 1)
-            if ahead:
-                quantize_x(b + 1, 1)
-            multiply(b, 2)
-            multiply(b, 3)
+        for b in range(2, B - 1):
+            plain_stretch(b)
+            prepare(b + 1)
+            for h in range(HALVES):
+                quantize_x(b + 1, h)
+            for n in range(CHUNKS):
+                multiply(b, n)
+
+        last = B - 1
+        plain_stretch(last)
+        multiply(last, 0)
+        multiply(last, 1)
+        run(lora_steps(last))
+        multiply(last, 2)
+        multiply(last, 3)

@@ -24,6 +24,7 @@ HALVES = 2
 HALF = 1024
 BANKS = 8
 PER_BANK = 4
+FIRST_ON_VECTOR = 3
 TAIL_WIDTHS = (256, 256)
 
 
@@ -49,6 +50,7 @@ def tile_linear_pa_kernel(tc, data, W_words, W_scales, t_lora, lora_b, out):
         make_identity(nc, ident_bf16[:])
 
         x_raw, b_raw, t_raw, t_T, w_codes, w_scales = {}, {}, {}, {}, {}, {}
+        x_pieces, x_turned = {}, {}
         x_split, b_paired, x_grouped, x_codes, x_scales, b_T, waiting = {}, {}, {}, {}, {}, {}, {}
 
         def load_x(b):
@@ -62,6 +64,13 @@ def tile_linear_pa_kernel(tc, data, W_words, W_scales, t_lora, lora_b, out):
                 tile = keep.tile([P, HALF], BF16, name="x_raw%d_%d" % (b, h))
                 nc.sync.dma_start(out=tile[:], in_=data[b, :, h * HALF : (h + 1) * HALF])
                 x_raw[b, h] = tile[:]
+
+        def load_x_by_quadrants(b):
+            tile = keep.tile([P, 4 * PASSES, P], BF16, name="x_raw%d" % b)
+            pieces = data[b].rearrange("(i t) (g q c) -> q i (t g) c", t=4, g=PASSES, q=4)
+            for q in (0, 2, 1, 3):
+                nc.sync.dma_start(out=tile[32 * q : 32 * (q + 1), :, :], in_=pieces[q])
+            x_pieces[b] = tile
 
         def load_b(b):
             tile = keep.tile([P, HALVES, HALF], BF16, name="b_raw%d" % b)
@@ -104,16 +113,38 @@ def tile_linear_pa_kernel(tc, data, W_words, W_scales, t_lora, lora_b, out):
             load_b(b)
             load_t(b)
             if b + 1 < B:
-                load_x(b + 1)
+                (load_x if b + 1 < FIRST_ON_VECTOR else load_x_by_quadrants)(b + 1)
 
         def split_x(b):
             for h in range(HALVES):
-                tile = stage.tile([P, HALF // 2], F32, name="x_split", tag="x_split")
+                tile = stage.tile([P, HALF // 2], F32, name="x_split", tag="x_split", align_bytes=64)
                 nc.vector.tensor_copy(
                     out=tile[:].rearrange("s (g u p) -> s g u p", g=2, u=2),
                     in_=x_raw[b, h].bitcast(F32).rearrange("s (g p u) -> s g u p", g=2, u=2),
                 )
                 x_split[b, h] = tile
+
+        def split_pieces(b, h, copy):
+            tile = stage.tile([P, HALF // 2], F32, name="x_split", tag="x_split", align_bytes=64)
+            words = x_pieces[b][:].bitcast(F32).rearrange("p (t g) (j u) -> p g t u j", g=PASSES, u=2)
+            copy(
+                out=tile[:].rearrange("p (g t u j) -> p g t u j", g=2, t=4, u=2),
+                in_=words[:, 2 * h : 2 * h + 2],
+            )
+            x_split[b, h] = tile
+
+        def turn_x(b, h):
+            tile = stage.tile([P, HALF // 2], F32, name="x_turned", tag="x_turned", align_bytes=64)
+            nc.vector.transpose(out=tile[:], in_=x_split[b, h][:])
+            x_turned[b, h] = tile
+
+        def regroup_x(b, h):
+            tile = stage.tile([P, HALF], BF16, name="x_grouped", tag="x_grouped", align_bytes=64)
+            dst = tile[:].bitcast(F32).rearrange("p (g i a w) -> p a g i w", g=2, a=2, w=4)
+            src = x_turned[b, h][:].rearrange("p (g a w i) -> p a g i w", g=2, a=2, w=4)
+            for a in range(2):
+                nc.scalar.copy(out=dst[:, a], in_=src[:, a])
+            x_grouped[b, h] = tile
 
         def pair_b(b):
             for h in range(HALVES):
@@ -182,7 +213,7 @@ def tile_linear_pa_kernel(tc, data, W_words, W_scales, t_lora, lora_b, out):
                 waiting[b, n] = tile
                 return
             other = waiting[b, n][:, lo:hi]
-            result = stage.tile([P, hi - lo], F32, name="result", tag="result", bufs=16)
+            result = stage.tile([P, hi - lo], F32, name="result", tag="result", bufs=24)
             nc.vector.scalar_tensor_tensor(
                 out=result[:],
                 in0=bank[:] if is_lora else other,
@@ -242,19 +273,20 @@ def tile_linear_pa_kernel(tc, data, W_words, W_scales, t_lora, lora_b, out):
             for step in steps:
                 step()
 
-        def plain_stretch(b):
-            transposes = transposes_b(b, 0) + transposes_t(b)
-            if b + 1 < B:
-                transposes += transposes_x(b + 1, 0)
-            transposes += transposes_b(b, 1)
-            if b + 1 < B:
-                transposes += transposes_x(b + 1, 1)
+        def plain_stretch(b, after_b):
+            on_tensor = b + 1 < FIRST_ON_VECTOR
+            transposes = []
+            for h in range(HALVES):
+                transposes += transposes_b(b, h)
+                if h == 0:
+                    transposes += transposes_t(b)
+                if on_tensor:
+                    transposes += transposes_x(b + 1, h)
+                transposes[-1] = partial(run, [transposes[-1], partial(after_b, h)])
             weave(lora_steps(b - 1), transposes, CHUNKS - 1)
 
-        def prepare(b):
-            pair_b(b)
-            if b + 1 < B:
-                split_x(b + 1)
+        def nothing(h):
+            return None
 
         split_x(0)
         run(transposes_x(0, 0) + transposes_x(0, 1))
@@ -269,26 +301,43 @@ def tile_linear_pa_kernel(tc, data, W_words, W_scales, t_lora, lora_b, out):
         multiply(0, 1)
         multiply(1, 1)
         run(transposes_b(0, 0) + transposes_t(0) + transposes_b(0, 1))
-        prepare(1)
+        pair_b(1)
+        split_x(2)
         multiply(0, 2)
         multiply(1, 2)
-        plain_stretch(1)
-        prepare(2)
+        plain_stretch(1, nothing)
+        pair_b(2)
         multiply(0, 3)
         for h in range(HALVES):
             quantize_x(2, h)
         multiply(1, 3)
 
         for b in range(2, B - 1):
-            plain_stretch(b)
-            prepare(b + 1)
-            for h in range(HALVES):
-                quantize_x(b + 1, h)
-            for n in range(CHUNKS):
-                multiply(b, n)
+            if b + 1 < FIRST_ON_VECTOR:
+                plain_stretch(b, nothing)
+                pair_b(b + 1)
+                if b + 2 < FIRST_ON_VECTOR:
+                    split_x(b + 2)
+                for h in range(HALVES):
+                    quantize_x(b + 1, h)
+                for n in range(CHUNKS):
+                    multiply(b, n)
+            else:
+                plain_stretch(b, partial(split_pieces, b + 1, copy=nc.scalar.copy))
+                for h in range(HALVES):
+                    turn_x(b + 1, h)
+                pair_b(b + 1)
+                multiply(b, 0)
+                regroup_x(b + 1, 0)
+                multiply(b, 1)
+                regroup_x(b + 1, 1)
+                for h in range(HALVES):
+                    quantize_x(b + 1, h)
+                multiply(b, 2)
+                multiply(b, 3)
 
         last = B - 1
-        plain_stretch(last)
+        plain_stretch(last, nothing)
         multiply(last, 0)
         multiply(last, 1)
         run(lora_steps(last))

@@ -17,22 +17,28 @@ E5M2X4 = mybir.dt.float8_e5m2_x4
 E2M1X4 = mybir.dt.float4_e2m1fn_x4
 
 P = 128
-PASSES = IN // 512
-N_TILE = 512
-CHUNKS = OUT // N_TILE
+QUADRANT = 32
+QUADRANTS = P // QUADRANT
+PASSES = IN // (4 * P)
+CHUNK = 512
+CHUNKS = OUT // CHUNK
 HALVES = 2
 HALF = 1024
 BANKS = 8
 PER_BANK = 4
-FIRST_ON_VECTOR = 3
-TAIL_WIDTHS = (256, 256)
+HEAD_ROWS = 2
+ROWS_TURNED_ON_VECTOR = (4, 6)
+LAST_WIDTHS = (256, 256)
+STAGE_BUFS = 4
+WAITING_BUFS = 10
+RESULT_BUFS = 24
 
 
 def tile_linear_pa_kernel(tc, data, W_words, W_scales, t_lora, lora_b, out):
     nc = tc.nc
     with ExitStack() as ctx:
         keep = ctx.enter_context(tc.tile_pool(name="keep", bufs=1))
-        stage = ctx.enter_context(tc.tile_pool(name="stage", bufs=4))
+        stage = ctx.enter_context(tc.tile_pool(name="stage", bufs=STAGE_BUFS))
         psum = ctx.enter_context(tc.psum_pool(name="psum", bufs=1))
         ctx.enter_context(tc.manual_schedule())
 
@@ -49,9 +55,10 @@ def tile_linear_pa_kernel(tc, data, W_words, W_scales, t_lora, lora_b, out):
         make_identity(nc, ident_f32[:])
         make_identity(nc, ident_bf16[:])
 
-        x_raw, b_raw, t_raw, t_T, w_codes, w_scales = {}, {}, {}, {}, {}, {}
-        x_pieces, x_turned = {}, {}
-        x_split, b_paired, x_grouped, x_codes, x_scales, b_T, waiting = {}, {}, {}, {}, {}, {}, {}
+        x_raw, x_pieces, b_raw, t_raw, w_codes, w_scales = {}, {}, {}, {}, {}, {}
+        x_split, x_turned, x_grouped, x_codes, x_scales = {}, {}, {}, {}, {}
+        b_paired, b_T, t_T, waiting = {}, {}, {}, {}
+
 
         def load_x(b):
             tile = keep.tile([P, IN], BF16, name="x_raw%d" % b)
@@ -66,54 +73,51 @@ def tile_linear_pa_kernel(tc, data, W_words, W_scales, t_lora, lora_b, out):
                 x_raw[b, h] = tile[:]
 
         def load_x_by_quadrants(b):
-            tile = keep.tile([P, 4 * PASSES, P], BF16, name="x_raw%d" % b)
-            pieces = data[b].rearrange("(i t) (g q c) -> q i (t g) c", t=4, g=PASSES, q=4)
+            tile = keep.tile([P, 4 * PASSES, P], BF16, name="x_pieces%d" % b)
+            pieces = data[b].rearrange("(i m) (g q c) -> q i (m g) c", m=4, g=PASSES, q=QUADRANTS)
             for q in (0, 2, 1, 3):
-                nc.sync.dma_start(out=tile[32 * q : 32 * (q + 1), :, :], in_=pieces[q])
+                nc.sync.dma_start(out=tile[QUADRANT * q : QUADRANT * (q + 1), :, :], in_=pieces[q])
             x_pieces[b] = tile
 
-        def load_b(b):
+        def load_adapter(b):
             tile = keep.tile([P, HALVES, HALF], BF16, name="b_raw%d" % b)
             nc.sync.dma_start(out=tile[:], in_=lora_b[b].rearrange("(h p x) r -> p h (x r)", h=HALVES, p=P))
             for h in range(HALVES):
                 b_raw[b, h] = tile[:, h, :]
+            t_tile = keep.tile([P, R], BF16, name="t_raw%d" % b)
+            nc.sync.dma_start(out=t_tile[:], in_=t_lora[b, 0])
+            t_raw[b] = t_tile
 
         def load_w(n):
-            plane = keep.tile([P, PASSES, N_TILE], U8, name="w_scales%d" % n, align_bytes=64)
-            cols = slice(n * N_TILE, (n + 1) * N_TILE)
+            scales = keep.tile([P, PASSES, CHUNK], U8, name="w_scales%d" % n, align_bytes=64)
             for r in range(4):
                 nc.sync.dma_start(
-                    out=plane[r:P:32, :, :].bitcast(I32),
-                    in_=W_scales[:, r:16:4, cols].rearrange("g q n -> q g n").bitcast(I32),
+                    out=scales[r:P:QUADRANT, :, :].bitcast(I32),
+                    in_=W_scales[:, r:16:4, n * CHUNK : (n + 1) * CHUNK].rearrange("g q n -> q g n").bitcast(I32),
                 )
-            words = keep.tile([P, PASSES, 2 * N_TILE], U8, name="w_codes%d" % n, align_bytes=64)
+            codes = keep.tile([P, PASSES, 2 * CHUNK], U8, name="w_codes%d" % n, align_bytes=64)
             nc.sync.dma_start(
-                out=words[:].bitcast(I32),
-                in_=W_words[:, :, 2 * n * N_TILE : 2 * (n + 1) * N_TILE].rearrange("g p c -> p g c").bitcast(I32),
+                out=codes[:].bitcast(I32),
+                in_=W_words[:, :, 2 * n * CHUNK : 2 * (n + 1) * CHUNK].rearrange("g p c -> p g c").bitcast(I32),
             )
-            w_scales[n], w_codes[n] = plane, words
-
-        def load_t(b):
-            tile = keep.tile([P, R], BF16, name="t_raw%d" % b)
-            nc.sync.dma_start(out=tile[:], in_=t_lora[b, 0])
-            t_raw[b] = tile
+            w_scales[n], w_codes[n] = scales, codes
 
         load_x_by_halves(0)
         load_x(1)
         load_w(0)
         load_w(1)
-        load_b(0)
-        load_t(0)
+        load_adapter(0)
         load_w(2)
-        load_b(1)
-        load_t(1)
+        load_adapter(1)
         load_x(2)
         load_w(3)
-        for b in range(2, B):
-            load_b(b)
-            load_t(b)
-            if b + 1 < B:
-                (load_x if b + 1 < FIRST_ON_VECTOR else load_x_by_quadrants)(b + 1)
+        for b in range(HEAD_ROWS, B):
+            load_adapter(b)
+            if b + 1 in ROWS_TURNED_ON_VECTOR:
+                load_x_by_quadrants(b + 1)
+            elif b + 1 < B:
+                load_x(b + 1)
+
 
         def split_x(b):
             for h in range(HALVES):
@@ -123,37 +127,6 @@ def tile_linear_pa_kernel(tc, data, W_words, W_scales, t_lora, lora_b, out):
                     in_=x_raw[b, h].bitcast(F32).rearrange("s (g p u) -> s g u p", g=2, u=2),
                 )
                 x_split[b, h] = tile
-
-        def split_pieces(b, h, copy):
-            tile = stage.tile([P, HALF // 2], F32, name="x_split", tag="x_split", align_bytes=64)
-            words = x_pieces[b][:].bitcast(F32).rearrange("p (t g) (j u) -> p g t u j", g=PASSES, u=2)
-            copy(
-                out=tile[:].rearrange("p (g t u j) -> p g t u j", g=2, t=4, u=2),
-                in_=words[:, 2 * h : 2 * h + 2],
-            )
-            x_split[b, h] = tile
-
-        def turn_x(b, h):
-            tile = stage.tile([P, HALF // 2], F32, name="x_turned", tag="x_turned", align_bytes=64)
-            nc.vector.transpose(out=tile[:], in_=x_split[b, h][:])
-            x_turned[b, h] = tile
-
-        def regroup_x(b, h):
-            tile = stage.tile([P, HALF], BF16, name="x_grouped", tag="x_grouped", align_bytes=64)
-            dst = tile[:].bitcast(F32).rearrange("p (g i a w) -> p a g i w", g=2, a=2, w=4)
-            src = x_turned[b, h][:].rearrange("p (g a w i) -> p a g i w", g=2, a=2, w=4)
-            for a in range(2):
-                nc.scalar.copy(out=dst[:, a], in_=src[:, a])
-            x_grouped[b, h] = tile
-
-        def pair_b(b):
-            for h in range(HALVES):
-                tile = stage.tile([P, HALF], BF16, name="b_paired", tag="b_paired")
-                nc.vector.tensor_copy(
-                    out=tile[:].rearrange("p (y r j) -> p y r j", y=PER_BANK, j=2),
-                    in_=b_raw[b, h].rearrange("p (y j r) -> p y r j", y=PER_BANK, j=2),
-                )
-                b_paired[b, h] = tile
 
         def word_transposes(words, empty):
             taken = []
@@ -179,6 +152,46 @@ def tile_linear_pa_kernel(tc, data, W_words, W_scales, t_lora, lora_b, out):
 
             return word_transposes(x_split[b, h][:], empty)
 
+
+        def split_pieces(b, h):
+            tile = stage.tile([P, HALF // 2], F32, name="x_split", tag="x_split", align_bytes=64)
+            words = x_pieces[b][:].bitcast(F32).rearrange("p (m g) (j u) -> p g m u j", g=PASSES, u=2)
+            nc.vector.tensor_copy(
+                out=tile[:].rearrange("p (g m u j) -> p g m u j", g=2, m=4, u=2),
+                in_=words[:, 2 * h : 2 * h + 2],
+            )
+            x_split[b, h] = tile
+
+        def turn_x(b, h):
+            tile = stage.tile([P, HALF // 2], F32, name="x_turned", tag="x_turned", align_bytes=64)
+            nc.vector.transpose(out=tile[:], in_=x_split[b, h][:])
+            x_turned[b, h] = tile
+
+        def regroup_x(b, h):
+            tile = stage.tile([P, HALF], BF16, name="x_grouped", tag="x_grouped", align_bytes=64)
+            dst = tile[:].bitcast(F32).rearrange("p (g i a w) -> p a g i w", g=2, a=2, w=4)
+            src = x_turned[b, h][:].rearrange("p (g a w i) -> p a g i w", g=2, a=2, w=4)
+            for a in range(2):
+                nc.scalar.copy(out=dst[:, a], in_=src[:, a])
+            x_grouped[b, h] = tile
+
+        def quantize_x(b):
+            for h in range(HALVES):
+                codes = stage.tile([P, HALF // 4], U32, name="x_codes", tag="x_codes", align_bytes=64)
+                scales = stage.tile([P, HALF // 4], U8, name="x_scales", tag="x_scales", align_bytes=64)
+                nc.vector.quantize_mx(out=codes[:].bitcast(E5M2X4), scales=scales[:], in_=x_grouped[b, h][:])
+                x_codes[b, h], x_scales[b, h] = codes, scales
+
+
+        def pair_b(b):
+            for h in range(HALVES):
+                tile = stage.tile([P, HALF], BF16, name="b_paired", tag="b_paired")
+                nc.vector.tensor_copy(
+                    out=tile[:].rearrange("p (y r j) -> p y r j", y=PER_BANK, j=2),
+                    in_=b_raw[b, h].rearrange("p (y j r) -> p y r j", y=PER_BANK, j=2),
+                )
+                b_paired[b, h] = tile
+
         def transposes_b(b, h):
             def empty(bank):
                 tile = stage.tile([P, HALF], BF16, name="b_T", tag="b_T")
@@ -190,156 +203,129 @@ def tile_linear_pa_kernel(tc, data, W_words, W_scales, t_lora, lora_b, out):
 
             return word_transposes(b_paired[b, h][:].bitcast(F32), empty)
 
-        def transposes_t(b):
-            def step():
-                bank = next_bank(S, BF16)
-                nc.tensor.transpose(bank[:], t_raw[b][:], ident_bf16[:])
-                tile = stage.tile([P, S], BF16, name="t_T", tag="t_T")
-                nc.scalar.copy(out=tile[:], in_=bank[:])
-                t_T[b] = tile
+        def transpose_t(b):
+            bank = next_bank(S, BF16)
+            nc.tensor.transpose(bank[:], t_raw[b][:], ident_bf16[:])
+            tile = stage.tile([P, S], BF16, name="t_T", tag="t_T")
+            nc.scalar.copy(out=tile[:], in_=bank[:])
+            t_T[b] = tile
 
-            return [step]
-
-        def quantize_x(b, h):
-            codes = stage.tile([P, HALF // 4], U32, name="x_codes", tag="x_codes", align_bytes=64)
-            scales = stage.tile([P, HALF // 4], U8, name="x_scales", tag="x_scales", align_bytes=64)
-            nc.vector.quantize_mx(out=codes[:].bitcast(E5M2X4), scales=scales[:], in_=x_grouped[b, h][:])
-            x_codes[b, h], x_scales[b, h] = codes, scales
 
         def deliver(b, n, lo, hi, bank, is_lora):
             if (b, n) not in waiting:
-                tile = stage.tile([P, N_TILE], F32, name="waiting", tag="waiting", bufs=10)
+                tile = stage.tile([P, CHUNK], F32, name="waiting", tag="waiting", bufs=WAITING_BUFS)
                 nc.scalar.copy(out=tile[:], in_=bank[:])
                 waiting[b, n] = tile
                 return
-            other = waiting[b, n][:, lo:hi]
-            result = stage.tile([P, hi - lo], F32, name="result", tag="result", bufs=24)
+            first = waiting[b, n][:, lo:hi]
+            result = stage.tile([P, hi - lo], F32, name="result", tag="result", bufs=RESULT_BUFS)
             nc.vector.scalar_tensor_tensor(
                 out=result[:],
-                in0=bank[:] if is_lora else other,
+                in0=bank[:] if is_lora else first,
                 scalar=SCALING,
-                in1=other if is_lora else bank[:],
+                in1=first if is_lora else bank[:],
                 op0=mybir.AluOpType.mult,
                 op1=mybir.AluOpType.add,
             )
-            nc.sync.dma_start(out=out[b, :, n * N_TILE + lo : n * N_TILE + hi], in_=result[:])
+            nc.sync.dma_start(out=out[b, :, n * CHUNK + lo : n * CHUNK + hi], in_=result[:])
 
         def lora_product(b, n):
-            bank = next_bank(N_TILE, F32)
+            bank = next_bank(CHUNK, F32)
             h, c = divmod(n, 2)
             nc.tensor.matmul(
-                bank[:],
-                lhsT=t_T[b][:],
-                rhs=b_T[b, h][:, c * N_TILE : (c + 1) * N_TILE],
-                start=True,
-                stop=True,
+                bank[:], lhsT=t_T[b][:], rhs=b_T[b, h][:, c * CHUNK : (c + 1) * CHUNK], start=True, stop=True
             )
-            deliver(b, n, 0, N_TILE, bank, True)
+            deliver(b, n, 0, CHUNK, bank, True)
 
-        def lora_steps(b):
-            return [partial(lora_product, b, n) for n in range(CHUNKS)]
+        def base_product(b, n):
+            lo = 0
+            for width in LAST_WIDTHS if (b, n) == (B - 1, CHUNKS - 1) else (CHUNK,):
+                hi = lo + width
+                bank = next_bank(width, F32)
+                for g in range(PASSES):
+                    h, c = divmod(g, 2)
+                    tokens = slice(c * S, (c + 1) * S)
+                    nc.tensor.matmul_mx(
+                        out=bank[:],
+                        lhsT=x_codes[b, h][:, tokens].bitcast(E5M2X4),
+                        lhsT_scale=x_scales[b, h][:, tokens],
+                        rhs=w_codes[n][:, g, 2 * lo : 2 * hi].bitcast(E2M1X4),
+                        rhs_scale=w_scales[n][:, g, lo:hi],
+                        start=(g == 0),
+                        stop=(g == PASSES - 1),
+                    )
+                deliver(b, n, lo, hi, bank, False)
+                lo = hi
 
-        def weave(matmuls, transposes, gaps):
-            for i, matmul in enumerate(matmuls):
-                matmul()
-                if i < gaps:
-                    for step in transposes[i * len(transposes) // gaps : (i + 1) * len(transposes) // gaps]:
+        def adapter_and_data_transposes(b, with_data):
+            steps = []
+            for h in range(HALVES):
+                steps += transposes_b(b, h)
+                if h == 0:
+                    steps.append(partial(transpose_t, b))
+                if with_data:
+                    steps += transposes_x(b + 1, h)
+            return steps
+
+        def plain_stretch(b):
+            steps = adapter_and_data_transposes(b, b + 1 < B and b + 1 not in ROWS_TURNED_ON_VECTOR)
+            gaps = CHUNKS - 1
+            for n in range(CHUNKS):
+                lora_product(b - 1, n)
+                if n < gaps:
+                    for step in steps[n * len(steps) // gaps : (n + 1) * len(steps) // gaps]:
                         step()
 
-        def base_product(b, n, lo, hi):
-            bank = next_bank(hi - lo, F32)
-            for g in range(PASSES):
-                h, c = divmod(g, 2)
-                cols = slice(c * S, (c + 1) * S)
-                nc.tensor.matmul_mx(
-                    out=bank[:],
-                    lhsT=x_codes[b, h][:, cols].bitcast(E5M2X4),
-                    lhsT_scale=x_scales[b, h][:, cols],
-                    rhs=w_codes[n][:, g, 2 * lo : 2 * hi].bitcast(E2M1X4),
-                    rhs_scale=w_scales[n][:, g, lo:hi],
-                    start=(g == 0),
-                    stop=(g == PASSES - 1),
-                )
-            return bank
-
-        def multiply(b, n):
-            widths = TAIL_WIDTHS if (b, n) == (B - 1, CHUNKS - 1) else (N_TILE,)
-            lo = 0
-            for width in widths:
-                deliver(b, n, lo, lo + width, base_product(b, n, lo, lo + width), False)
-                lo += width
-
-        def run(steps):
-            for step in steps:
-                step()
-
-        def plain_stretch(b, after_b):
-            on_tensor = b + 1 < FIRST_ON_VECTOR
-            transposes = []
+        for b in range(HEAD_ROWS):
+            split_x(b)
             for h in range(HALVES):
-                transposes += transposes_b(b, h)
-                if h == 0:
-                    transposes += transposes_t(b)
-                if on_tensor:
-                    transposes += transposes_x(b + 1, h)
-                transposes[-1] = partial(run, [transposes[-1], partial(after_b, h)])
-            weave(lora_steps(b - 1), transposes, CHUNKS - 1)
-
-        def nothing(h):
-            return None
-
-        split_x(0)
-        run(transposes_x(0, 0) + transposes_x(0, 1))
-        split_x(1)
-        run(transposes_x(1, 0) + transposes_x(1, 1))
-        for b in range(2):
-            for h in range(HALVES):
-                quantize_x(b, h)
-        multiply(0, 0)
-        multiply(1, 0)
+                for step in transposes_x(b, h):
+                    step()
+        for b in range(HEAD_ROWS):
+            quantize_x(b)
+        base_product(0, 0)
+        base_product(1, 0)
         pair_b(0)
-        multiply(0, 1)
-        multiply(1, 1)
-        run(transposes_b(0, 0) + transposes_t(0) + transposes_b(0, 1))
+        base_product(0, 1)
+        base_product(1, 1)
+        for step in adapter_and_data_transposes(0, False):
+            step()
         pair_b(1)
         split_x(2)
-        multiply(0, 2)
-        multiply(1, 2)
-        plain_stretch(1, nothing)
+        base_product(0, 2)
+        base_product(1, 2)
+        plain_stretch(1)
         pair_b(2)
-        multiply(0, 3)
-        for h in range(HALVES):
-            quantize_x(2, h)
-        multiply(1, 3)
+        split_x(3)
+        base_product(0, 3)
+        quantize_x(2)
+        base_product(1, 3)
 
-        for b in range(2, B - 1):
-            if b + 1 < FIRST_ON_VECTOR:
-                plain_stretch(b, nothing)
-                pair_b(b + 1)
-                if b + 2 < FIRST_ON_VECTOR:
-                    split_x(b + 2)
-                for h in range(HALVES):
-                    quantize_x(b + 1, h)
-                for n in range(CHUNKS):
-                    multiply(b, n)
-            else:
-                plain_stretch(b, partial(split_pieces, b + 1, copy=nc.scalar.copy))
-                for h in range(HALVES):
-                    turn_x(b + 1, h)
-                pair_b(b + 1)
-                multiply(b, 0)
+        for b in range(HEAD_ROWS, B - 1):
+            plain_stretch(b)
+            if b + 1 in ROWS_TURNED_ON_VECTOR:
+                split_pieces(b + 1, 1)
+                turn_x(b + 1, 1)
                 regroup_x(b + 1, 0)
-                multiply(b, 1)
+            pair_b(b + 1)
+            if b + 2 in ROWS_TURNED_ON_VECTOR:
+                split_pieces(b + 2, 0)
+            elif b + 2 < B:
+                split_x(b + 2)
+            base_product(b, 0)
+            if b + 1 in ROWS_TURNED_ON_VECTOR:
                 regroup_x(b + 1, 1)
-                for h in range(HALVES):
-                    quantize_x(b + 1, h)
-                multiply(b, 2)
-                multiply(b, 3)
+            quantize_x(b + 1)
+            if b + 2 in ROWS_TURNED_ON_VECTOR:
+                turn_x(b + 2, 0)
+            for n in range(1, CHUNKS):
+                base_product(b, n)
 
         last = B - 1
-        plain_stretch(last, nothing)
-        multiply(last, 0)
-        multiply(last, 1)
-        run(lora_steps(last))
-        multiply(last, 2)
-        multiply(last, 3)
+        plain_stretch(last)
+        for n in range(CHUNKS // 2):
+            base_product(last, n)
+        for n in range(CHUNKS):
+            lora_product(last, n)
+        for n in range(CHUNKS // 2, CHUNKS):
+            base_product(last, n)

from contextlib import ExitStack
from functools import partial

import concourse.mybir as mybir
from concourse.masks import make_identity

B, S, IN, OUT, R = 8, 128, 2048, 2048, 128
SCALING = 2.0
FLOPS = 2 * B * S * IN * OUT + 2 * B * S * R * OUT

F32 = mybir.dt.float32
BF16 = mybir.dt.bfloat16
I32 = mybir.dt.int32
U32 = mybir.dt.uint32
U8 = mybir.dt.uint8
E5M2X4 = mybir.dt.float8_e5m2_x4
E2M1X4 = mybir.dt.float4_e2m1fn_x4

P = 128
QUADRANT = 32
QUADRANTS = P // QUADRANT
PASSES = IN // (4 * P)
CHUNK = 512
CHUNKS = OUT // CHUNK
HALVES = 2
HALF = 1024
BANKS = 8
PER_BANK = 4
HEAD_ROWS = 2
ROWS_TURNED_ON_VECTOR = (4, 6)
LAST_WIDTHS = (256, 256)
STAGE_BUFS = 4
WAITING_BUFS = 10
RESULT_BUFS = 24


def tile_linear_pa_kernel(tc, data, W_words, W_scales, t_lora, lora_b, out):
    nc = tc.nc
    with ExitStack() as ctx:
        keep = ctx.enter_context(tc.tile_pool(name="keep", bufs=1))
        stage = ctx.enter_context(tc.tile_pool(name="stage", bufs=STAGE_BUFS))
        psum = ctx.enter_context(tc.psum_pool(name="psum", bufs=1))
        ctx.enter_context(tc.manual_schedule())

        banks_taken = []

        def next_bank(width, dtype):
            tag = "bank%d" % (len(banks_taken) % BANKS)
            bank = psum.tile([P, width], dtype, name=tag, tag=tag)
            banks_taken.append(tag)
            return bank

        ident_f32 = keep.tile([P, P], F32, name="ident_f32")
        ident_bf16 = keep.tile([P, P], BF16, name="ident_bf16")
        make_identity(nc, ident_f32[:])
        make_identity(nc, ident_bf16[:])

        x_raw, x_pieces, b_raw, t_raw, w_codes, w_scales = {}, {}, {}, {}, {}, {}
        x_split, x_turned, x_grouped, x_codes, x_scales = {}, {}, {}, {}, {}
        b_paired, b_T, t_T, waiting = {}, {}, {}, {}


        def load_x(b):
            tile = keep.tile([P, IN], BF16, name="x_raw%d" % b)
            nc.sync.dma_start(out=tile[:], in_=data[b])
            for h in range(HALVES):
                x_raw[b, h] = tile[:, h * HALF : (h + 1) * HALF]

        def load_x_by_halves(b):
            for h in range(HALVES):
                tile = keep.tile([P, HALF], BF16, name="x_raw%d_%d" % (b, h))
                nc.sync.dma_start(out=tile[:], in_=data[b, :, h * HALF : (h + 1) * HALF])
                x_raw[b, h] = tile[:]

        def load_x_by_quadrants(b):
            tile = keep.tile([P, 4 * PASSES, P], BF16, name="x_pieces%d" % b)
            pieces = data[b].rearrange("(i m) (g q c) -> q i (m g) c", m=4, g=PASSES, q=QUADRANTS)
            for q in (0, 2, 1, 3):
                nc.sync.dma_start(out=tile[QUADRANT * q : QUADRANT * (q + 1), :, :], in_=pieces[q])
            x_pieces[b] = tile

        def load_adapter(b):
            tile = keep.tile([P, HALVES, HALF], BF16, name="b_raw%d" % b)
            nc.sync.dma_start(out=tile[:], in_=lora_b[b].rearrange("(h p x) r -> p h (x r)", h=HALVES, p=P))
            for h in range(HALVES):
                b_raw[b, h] = tile[:, h, :]
            t_tile = keep.tile([P, R], BF16, name="t_raw%d" % b)
            nc.sync.dma_start(out=t_tile[:], in_=t_lora[b, 0])
            t_raw[b] = t_tile

        def load_w(n):
            scales = keep.tile([P, PASSES, CHUNK], U8, name="w_scales%d" % n, align_bytes=64)
            for r in range(4):
                nc.sync.dma_start(
                    out=scales[r:P:QUADRANT, :, :].bitcast(I32),
                    in_=W_scales[:, r:16:4, n * CHUNK : (n + 1) * CHUNK].rearrange("g q n -> q g n").bitcast(I32),
                )
            codes = keep.tile([P, PASSES, 2 * CHUNK], U8, name="w_codes%d" % n, align_bytes=64)
            nc.sync.dma_start(
                out=codes[:].bitcast(I32),
                in_=W_words[:, :, 2 * n * CHUNK : 2 * (n + 1) * CHUNK].rearrange("g p c -> p g c").bitcast(I32),
            )
            w_scales[n], w_codes[n] = scales, codes

        load_x_by_halves(0)
        load_x(1)
        load_w(0)
        load_w(1)
        load_adapter(0)
        load_w(2)
        load_adapter(1)
        load_x(2)
        load_w(3)
        for b in range(HEAD_ROWS, B):
            load_adapter(b)
            if b + 1 in ROWS_TURNED_ON_VECTOR:
                load_x_by_quadrants(b + 1)
            elif b + 1 < B:
                load_x(b + 1)


        def split_x(b):
            for h in range(HALVES):
                tile = stage.tile([P, HALF // 2], F32, name="x_split", tag="x_split", align_bytes=64)
                nc.vector.tensor_copy(
                    out=tile[:].rearrange("s (g u p) -> s g u p", g=2, u=2),
                    in_=x_raw[b, h].bitcast(F32).rearrange("s (g p u) -> s g u p", g=2, u=2),
                )
                x_split[b, h] = tile

        def word_transposes(words, empty):
            taken = []

            def step(i):
                if i == 0:
                    taken.append(next_bank(PER_BANK * P, F32))
                bank = taken[0]
                nc.tensor.transpose(bank[:, i * P : (i + 1) * P], words[:, i * P : (i + 1) * P], ident_f32[:])
                if i == PER_BANK - 1:
                    empty(bank)

            return [partial(step, i) for i in range(PER_BANK)]

        def transposes_x(b, h):
            def empty(bank):
                tile = stage.tile([P, HALF], BF16, name="x_grouped", tag="x_grouped", align_bytes=64)
                nc.scalar.copy(
                    out=tile[:].bitcast(F32).rearrange("p (g s u) -> p g s u", g=2, u=2),
                    in_=bank[:].rearrange("p (g u s) -> p g s u", g=2, u=2),
                )
                x_grouped[b, h] = tile

            return word_transposes(x_split[b, h][:], empty)


        def split_pieces(b, h):
            tile = stage.tile([P, HALF // 2], F32, name="x_split", tag="x_split", align_bytes=64)
            words = x_pieces[b][:].bitcast(F32).rearrange("p (m g) (j u) -> p g m u j", g=PASSES, u=2)
            nc.vector.tensor_copy(
                out=tile[:].rearrange("p (g m u j) -> p g m u j", g=2, m=4, u=2),
                in_=words[:, 2 * h : 2 * h + 2],
            )
            x_split[b, h] = tile

        def turn_x(b, h):
            tile = stage.tile([P, HALF // 2], F32, name="x_turned", tag="x_turned", align_bytes=64)
            nc.vector.transpose(out=tile[:], in_=x_split[b, h][:])
            x_turned[b, h] = tile

        def regroup_x(b, h):
            tile = stage.tile([P, HALF], BF16, name="x_grouped", tag="x_grouped", align_bytes=64)
            dst = tile[:].bitcast(F32).rearrange("p (g i a w) -> p a g i w", g=2, a=2, w=4)
            src = x_turned[b, h][:].rearrange("p (g a w i) -> p a g i w", g=2, a=2, w=4)
            for a in range(2):
                nc.scalar.copy(out=dst[:, a], in_=src[:, a])
            x_grouped[b, h] = tile

        def quantize_x(b):
            for h in range(HALVES):
                codes = stage.tile([P, HALF // 4], U32, name="x_codes", tag="x_codes", align_bytes=64)
                scales = stage.tile([P, HALF // 4], U8, name="x_scales", tag="x_scales", align_bytes=64)
                nc.vector.quantize_mx(out=codes[:].bitcast(E5M2X4), scales=scales[:], in_=x_grouped[b, h][:])
                x_codes[b, h], x_scales[b, h] = codes, scales


        def pair_b(b):
            for h in range(HALVES):
                tile = stage.tile([P, HALF], BF16, name="b_paired", tag="b_paired")
                nc.vector.tensor_copy(
                    out=tile[:].rearrange("p (y r j) -> p y r j", y=PER_BANK, j=2),
                    in_=b_raw[b, h].rearrange("p (y j r) -> p y r j", y=PER_BANK, j=2),
                )
                b_paired[b, h] = tile

        def transposes_b(b, h):
            def empty(bank):
                tile = stage.tile([P, HALF], BF16, name="b_T", tag="b_T")
                nc.scalar.copy(
                    out=tile[:].bitcast(F32).rearrange("r (p y) -> r p y", y=PER_BANK),
                    in_=bank[:].rearrange("r (y p) -> r p y", y=PER_BANK),
                )
                b_T[b, h] = tile

            return word_transposes(b_paired[b, h][:].bitcast(F32), empty)

        def transpose_t(b):
            bank = next_bank(S, BF16)
            nc.tensor.transpose(bank[:], t_raw[b][:], ident_bf16[:])
            tile = stage.tile([P, S], BF16, name="t_T", tag="t_T")
            nc.scalar.copy(out=tile[:], in_=bank[:])
            t_T[b] = tile


        def deliver(b, n, lo, hi, bank, is_lora):
            if (b, n) not in waiting:
                tile = stage.tile([P, CHUNK], F32, name="waiting", tag="waiting", bufs=WAITING_BUFS)
                nc.scalar.copy(out=tile[:], in_=bank[:])
                waiting[b, n] = tile
                return
            first = waiting[b, n][:, lo:hi]
            result = stage.tile([P, hi - lo], F32, name="result", tag="result", bufs=RESULT_BUFS)
            nc.vector.scalar_tensor_tensor(
                out=result[:],
                in0=bank[:] if is_lora else first,
                scalar=SCALING,
                in1=first if is_lora else bank[:],
                op0=mybir.AluOpType.mult,
                op1=mybir.AluOpType.add,
            )
            nc.sync.dma_start(out=out[b, :, n * CHUNK + lo : n * CHUNK + hi], in_=result[:])

        def lora_product(b, n):
            bank = next_bank(CHUNK, F32)
            h, c = divmod(n, 2)
            nc.tensor.matmul(
                bank[:], lhsT=t_T[b][:], rhs=b_T[b, h][:, c * CHUNK : (c + 1) * CHUNK], start=True, stop=True
            )
            deliver(b, n, 0, CHUNK, bank, True)

        def base_product(b, n):
            lo = 0
            for width in LAST_WIDTHS if (b, n) == (B - 1, CHUNKS - 1) else (CHUNK,):
                hi = lo + width
                bank = next_bank(width, F32)
                for g in range(PASSES):
                    h, c = divmod(g, 2)
                    tokens = slice(c * S, (c + 1) * S)
                    nc.tensor.matmul_mx(
                        out=bank[:],
                        lhsT=x_codes[b, h][:, tokens].bitcast(E5M2X4),
                        lhsT_scale=x_scales[b, h][:, tokens],
                        rhs=w_codes[n][:, g, 2 * lo : 2 * hi].bitcast(E2M1X4),
                        rhs_scale=w_scales[n][:, g, lo:hi],
                        start=(g == 0),
                        stop=(g == PASSES - 1),
                    )
                deliver(b, n, lo, hi, bank, False)
                lo = hi

        def adapter_and_data_transposes(b, with_data):
            steps = []
            for h in range(HALVES):
                steps += transposes_b(b, h)
                if h == 0:
                    steps.append(partial(transpose_t, b))
                if with_data:
                    steps += transposes_x(b + 1, h)
            return steps

        def plain_stretch(b):
            steps = adapter_and_data_transposes(b, b + 1 < B and b + 1 not in ROWS_TURNED_ON_VECTOR)
            gaps = CHUNKS - 1
            for n in range(CHUNKS):
                lora_product(b - 1, n)
                if n < gaps:
                    for step in steps[n * len(steps) // gaps : (n + 1) * len(steps) // gaps]:
                        step()

        for b in range(HEAD_ROWS):
            split_x(b)
            for h in range(HALVES):
                for step in transposes_x(b, h):
                    step()
        for b in range(HEAD_ROWS):
            quantize_x(b)
        base_product(0, 0)
        base_product(1, 0)
        pair_b(0)
        base_product(0, 1)
        base_product(1, 1)
        for step in adapter_and_data_transposes(0, False):
            step()
        pair_b(1)
        split_x(2)
        base_product(0, 2)
        base_product(1, 2)
        plain_stretch(1)
        pair_b(2)
        split_x(3)
        base_product(0, 3)
        quantize_x(2)
        base_product(1, 3)

        for b in range(HEAD_ROWS, B - 1):
            plain_stretch(b)
            if b + 1 in ROWS_TURNED_ON_VECTOR:
                split_pieces(b + 1, 1)
                turn_x(b + 1, 1)
                regroup_x(b + 1, 0)
            pair_b(b + 1)
            if b + 2 in ROWS_TURNED_ON_VECTOR:
                split_pieces(b + 2, 0)
            elif b + 2 < B:
                split_x(b + 2)
            base_product(b, 0)
            if b + 1 in ROWS_TURNED_ON_VECTOR:
                regroup_x(b + 1, 1)
            quantize_x(b + 1)
            if b + 2 in ROWS_TURNED_ON_VECTOR:
                turn_x(b + 2, 0)
            for n in range(1, CHUNKS):
                base_product(b, n)

        last = B - 1
        plain_stretch(last)
        for n in range(CHUNKS // 2):
            base_product(last, n)
        for n in range(CHUNKS):
            lora_product(last, n)
        for n in range(CHUNKS // 2, CHUNKS):
            base_product(last, n)
